import numpy as np
import ml_dtypes


def mxq(x, axis, fmt="e4m3"):
    dtype, down = {"e4m3": (ml_dtypes.float8_e4m3fn, 7), "e5m2": (ml_dtypes.float8_e5m2, 14)}[fmt]
    v = np.moveaxis(np.asarray(x, np.float32).astype(ml_dtypes.bfloat16).astype(np.float64), axis, -1)
    blocks = v.reshape(v.shape[:-1] + (-1, 32))
    amax = np.abs(blocks).max(-1, keepdims=True)
    byte = np.maximum(np.where(amax > 0, np.frexp(amax)[1] - 1 + 127, 0) - down, 1)
    scale = np.exp2(byte - 127.0)
    codes = (blocks / scale).astype(np.float32).astype(dtype).astype(np.float64)
    return np.moveaxis((codes * scale).reshape(v.shape), -1, axis)


WIDE = False


def mx_kscale(k):
    if not WIDE:
        return np.ones(k)
    levels = np.array([10, -10, 5, -5, 0])
    a = np.random.permutation(np.resize(levels, k // 512 * 4)).reshape(k // 512, 4)
    idx = np.arange(k)
    return np.exp2(a[idx // 512, idx % 128 // 32])


BF16 = ml_dtypes.bfloat16


def bf(x):
    return np.asarray(x, np.float32).astype(BF16)


def f64(x):
    return np.asarray(x).astype(np.float64)


B, N, P, D, H = 2, 512, 4, 256, 8
E = P * D
DH = E // H


def sincos_table(n, e):
    pe = np.zeros((n, e))
    position = np.arange(n, dtype=np.float64)[:, None]
    div_term = np.exp(np.arange(0, e, 2, dtype=np.float64) * -(np.log(10000.0) / e))
    pe[:, 0::2] = np.sin(position * div_term)
    pe[:, 1::2] = np.cos(position * div_term)
    pe = pe - pe.mean()
    return pe / (pe.std() * 10)


def setup_inputs():
    s, t = mx_kscale(E), mx_kscale(E)
    c = 1.0 / np.sqrt(E)
    return {"x": bf(np.random.standard_normal((B, N, P, D)) * s.reshape(P, D)),
            "pos_embed": bf(sincos_table(N, E) * t),
            "W_embed": bf(np.random.standard_normal((E, E)) * c * t[:, None] / s),
            "b_embed": bf(np.random.standard_normal(E) * 0.1 * t),
            "Wq": bf(np.random.standard_normal((E, E)) * c / t),
            "bq": bf(np.random.standard_normal(E) * 0.1),
            "Wk": bf(np.random.standard_normal((E, E)) * c / t),
            "bk": bf(np.random.standard_normal(E) * 0.1),
            "Wv": bf(np.random.standard_normal((E, E)) * c / t),
            "bv": bf(np.random.standard_normal(E) * 0.1)}


def reference(x, pos_embed, W_embed, b_embed, Wq, bq, Wk, bk, Wv, bv):
    xf = f64(x).reshape(B, N, E)
    xe = (mxq(xf, 2, "e4m3") @ mxq(f64(W_embed).T, 0, "e4m3")) + f64(b_embed)
    xe = xe + f64(pos_embed)
    xq = mxq(xe, 2, "e4m3")
    q = ((xq @ mxq(f64(Wq).T, 0, "e4m3")) + f64(bq)).reshape(B, N, H, DH)
    k = ((xq @ mxq(f64(Wk).T, 0, "e4m3")) + f64(bk)).reshape(B, N, H, DH)
    v = ((xq @ mxq(f64(Wv).T, 0, "e4m3")) + f64(bv)).reshape(B, N, H, DH)
    return q, k, v

@@ -1,0 +1,301 @@
+from contextlib import ExitStack
+
+import concourse.mybir as mybir
+from concourse.masks import make_identity
+
+BF16 = mybir.dt.bfloat16
+F32 = mybir.dt.float32
+U32 = mybir.dt.uint32
+U8 = mybir.dt.uint8
+FP8X4 = mybir.dt.float8_e4m3fn_x4
+ADD = mybir.AluOpType.add
+IDENTITY = mybir.ActivationFunctionType.Identity
+
+P = 128
+PACK = 4
+K_PASS = P * PACK
+E = 1024
+PASSES = E // K_PASS
+POSITIONS = 512
+TOKENS = 2 * POSITIONS
+ROW_TILES = 8
+HALF = ROW_TILES // 2
+WORDS = E // 2
+BANK = 512
+LANE_TOKENS = 4
+
+FLOPS = 4 * 2 * TOKENS * E * E
+
+
+def transpose_half(nc, psum, stage, raw, first_tile, ident, copies):
+    raw_words = raw[:].bitcast(F32)
+    banks = {}
+    for pair in range(HALF // 2):
+        for g in range(PASSES):
+            bank = psum.tile([P, 2, 2, P], F32, tag="transposed")
+            for i in range(2):
+                for u in range(2):
+                    first_word = (first_tile + 2 * pair + i) * WORDS + (2 * g + u) * P
+                    nc.tensor.transpose(
+                        bank[:, i, u, :], raw_words[:, first_word : first_word + P], ident[:]
+                    )
+            banks[(pair, g)] = bank
+    grouped_tiles = {}
+    for number, key in enumerate(sorted(banks)):
+        grouped = stage.tile([P, 2 * P * PACK], BF16, tag="grouped", align_bytes=64)
+        copy = copies[number % len(copies)]
+        copy(
+            out=grouped[:].bitcast(F32).rearrange("p (i r u) -> p i r u", i=2, u=2),
+            in_=banks[key][:].rearrange("p i u r -> p i r u"),
+        )
+        grouped_tiles[key] = grouped
+    return grouped_tiles
+
+
+def quantise_half(nc, grouped_tiles, first_tile, codes, scales):
+    for pair, g in sorted(grouped_tiles):
+        first = (first_tile + 2 * pair) * P
+        nc.vector.quantize_mx(
+            out=codes[:, g, first : first + 2 * P].bitcast(FP8X4),
+            scales=scales[:, g, first : first + 2 * P],
+            in_=grouped_tiles[(pair, g)][:],
+        )
+
+
+def tile_attention_pa_kernel(
+    tc, x, pos_embed, W_embed, b_embed, Wq, bq, Wk, bk, Wv, bv, out_0, out_1, out_2
+):
+    nc = tc.nc
+    weights = (Wq, Wk, Wv)
+    biases = (bq, bk, bv)
+
+    x_view = x.rearrange("b (r j) s d -> b r (j s d)", j=LANE_TOKENS)
+    pos_view = pos_embed.rearrange("(r j) e -> r j e", j=LANE_TOKENS)
+    out_views = [
+        out.rearrange("b (r j) h d -> b j r (h d)", j=LANE_TOKENS) for out in (out_0, out_1, out_2)
+    ]
+    w_embed_view = W_embed.rearrange("(a r e) k -> r a (e k)", r=P, e=2)
+    weight_views = [w.rearrange("(i r) k -> r i k", r=P) for w in weights]
+
+    with ExitStack() as ctx:
+        consts = ctx.enter_context(tc.tile_pool(name="consts", bufs=1))
+        raws = ctx.enter_context(tc.tile_pool(name="raws", bufs=3))
+        keep = ctx.enter_context(tc.tile_pool(name="keep", bufs=1))
+        stage = ctx.enter_context(tc.tile_pool(name="stage", bufs=8))
+        outs = ctx.enter_context(tc.tile_pool(name="outs", bufs=6))
+        psum = ctx.enter_context(tc.psum_pool(name="psum", bufs=4))
+
+        ident = consts.tile([P, P], F32)
+        make_identity(nc, ident[:])
+        ones = consts.tile([P, P], BF16)
+        nc.vector.memset(ones[:], 1.0)
+        bias_rows = consts.tile([P, 3 * E], BF16)
+        nc.vector.memset(bias_rows[:], 0.0)
+        b_embed_bf = consts.tile([P, HALF, 2], BF16)
+        nc.scalar.dma_start(out=b_embed_bf[:], in_=b_embed.rearrange("(a r e) -> r a e", r=P, e=2))
+        b_embed_f32 = consts.tile([P, ROW_TILES], F32)
+        nc.scalar.activation(
+            out=b_embed_f32[:], in_=b_embed_bf[:].rearrange("p a e -> p (a e)"), func=IDENTITY
+        )
+
+        w_embed_raw = raws.tile([P, ROW_TILES * E], BF16, tag="raw")
+        x_raw = raws.tile([P, ROW_TILES * E], BF16, tag="raw")
+        wq_raw = raws.tile([P, ROW_TILES * E], BF16, tag="raw")
+        pos_raw = consts.tile([P, LANE_TOKENS, E], BF16)
+
+        def load_w_embed(a):
+            nc.sync.dma_start(
+                out=w_embed_raw[:, 2 * a * E : 2 * (a + 1) * E], in_=w_embed_view[:, a, :]
+            )
+
+        def load_x(b, first_j, count):
+            first = (b * LANE_TOKENS + first_j) * E
+            nc.sync.dma_start(
+                out=x_raw[:, first : first + count * E],
+                in_=x_view[b][:, first_j * E : (first_j + count) * E],
+            )
+
+        def load_pos(g_out):
+            cols = slice(g_out * K_PASS, (g_out + 1) * K_PASS)
+            nc.sync.dma_start(out=pos_raw[:, :, cols], in_=pos_view[:, :, cols])
+
+        def load_weight(raw, w, half):
+            nc.sync.dma_start(
+                out=raw[:, half * HALF * E : (half + 1) * HALF * E].rearrange(
+                    "p (i k) -> p i k", i=HALF
+                ),
+                in_=weight_views[w][:, half * HALF : (half + 1) * HALF, :],
+            )
+
+        load_w_embed(0)
+        load_w_embed(1)
+        load_x(0, 0, 2)
+        load_x(0, 2, 2)
+        load_pos(0)
+        load_x(1, 0, LANE_TOKENS)
+        load_w_embed(2)
+        load_w_embed(3)
+        load_pos(1)
+        for w, bias in enumerate(biases):
+            nc.sync.dma_start(
+                out=bias_rows[0:1, w * E : (w + 1) * E], in_=bias.rearrange("(o f) -> o f", o=1)
+            )
+        load_weight(wq_raw, 0, 0)
+        load_weight(wq_raw, 0, 1)
+
+        def mx_operand(name):
+            codes = keep.tile([P, PASSES, E], U32, name=name + "_codes", align_bytes=64)
+            scales = keep.tile([P, PASSES, E], U8, name=name + "_scales", align_bytes=64)
+            return codes, scales
+
+        x_codes, x_scales = mx_operand("x")
+        we_codes, we_scales = mx_operand("w_embed")
+        xe_codes, xe_scales = mx_operand("xe")
+        w_mx = [mx_operand(name) for name in ("wq", "wk", "wv")]
+
+        both = (nc.scalar.copy, nc.vector.tensor_copy)
+        scalar_only = (nc.scalar.copy,)
+
+        pos_planes = consts.tile([P, ROW_TILES, POSITIONS], F32)
+
+        def transpose_pos(g_out):
+            for a in range(2 * g_out, 2 * g_out + 2):
+                bank = psum.tile([P, LANE_TOKENS, P], F32, tag="transposed")
+                for j in range(LANE_TOKENS):
+                    nc.tensor.transpose(
+                        bank[:, j, :], pos_raw[:, j, :].bitcast(F32)[:, a * P : (a + 1) * P], ident[:]
+                    )
+                pairs = (
+                    bank[:]
+                    .rearrange("p j r -> p (j r)")
+                    .bitcast(BF16)
+                    .rearrange("p (c e) -> p c e", e=2)
+                )
+                for e in range(2):
+                    plane = 2 * a + e
+                    nc.scalar.activation(
+                        out=pos_planes[:, plane, :],
+                        in_=pairs[:, :, e],
+                        func=IDENTITY,
+                        bias=b_embed_f32[:, plane : plane + 1],
+                        scale=1.0,
+                    )
+
+        xe_grouped = keep.tile([P, PASSES, TOKENS * PACK], BF16, align_bytes=64)
+
+        def embed(g_out, b):
+            for j in range(LANE_TOKENS):
+                first_token = (LANE_TOKENS * b + j) * P
+                tokens = slice(first_token, first_token + P)
+                acc = psum.tile([P, PACK, P], F32, tag="acc")
+                for t in range(PACK):
+                    features = slice((PACK * g_out + t) * P, (PACK * g_out + t + 1) * P)
+                    for g in range(PASSES):
+                        nc.tensor.matmul_mx(
+                            out=acc[:, t, :],
+                            lhsT=we_codes[:, g, features].bitcast(FP8X4),
+                            lhsT_scale=we_scales[:, g, features],
+                            rhs=x_codes[:, g, tokens].bitcast(FP8X4),
+                            rhs_scale=x_scales[:, g, tokens],
+                            start=(g == 0),
+                            stop=(g == PASSES - 1),
+                        )
+                nc.vector.tensor_tensor(
+                    out=xe_grouped[
+                        :, g_out, first_token * PACK : (first_token + P) * PACK
+                    ].rearrange("p (r t) -> p r t", t=PACK),
+                    in0=acc[:].rearrange("p t r -> p r t"),
+                    in1=pos_planes[
+                        :, PACK * g_out : PACK * (g_out + 1), j * P : (j + 1) * P
+                    ].rearrange("p t r -> p r t"),
+                    op=ADD,
+                )
+            batch = slice(b * POSITIONS, (b + 1) * POSITIONS)
+            nc.vector.quantize_mx(
+                out=xe_codes[:, g_out, batch].bitcast(FP8X4),
+                scales=xe_scales[:, g_out, batch],
+                in_=xe_grouped[:, g_out, b * POSITIONS * PACK : (b + 1) * POSITIONS * PACK],
+            )
+
+        bias_all = consts.tile([P, 3 * E], F32)
+
+        def spread_bias(w):
+            for h in range(E // BANK):
+                cols = slice(w * E + h * BANK, w * E + (h + 1) * BANK)
+                spread = psum.tile([P, BANK], F32, tag="acc")
+                nc.tensor.matmul(
+                    spread[:], lhsT=ones[:], rhs=bias_rows[:, cols], start=True, stop=True
+                )
+                nc.scalar.copy(out=bias_all[:, cols], in_=spread[:])
+
+        def project(w, tile_index):
+            codes, scales = w_mx[w]
+            tokens = slice(tile_index * P, (tile_index + 1) * P)
+            result = outs.tile([P, E], F32, tag="result")
+            for h in range(E // BANK):
+                features = slice(h * BANK, (h + 1) * BANK)
+                bias = bias_all[:, w * E + h * BANK : w * E + (h + 1) * BANK]
+                acc = psum.tile([P, BANK], F32, tag="acc")
+                for g in range(PASSES):
+                    nc.tensor.matmul_mx(
+                        out=acc[:],
+                        lhsT=xe_codes[:, g, tokens].bitcast(FP8X4),
+                        lhsT_scale=xe_scales[:, g, tokens],
+                        rhs=codes[:, g, features].bitcast(FP8X4),
+                        rhs_scale=scales[:, g, features],
+                        start=(g == 0),
+                        stop=(g == PASSES - 1),
+                    )
+                bank_number = (w * ROW_TILES + tile_index) * (E // BANK) + h
+                if bank_number % 3 == 0:
+                    nc.scalar.copy(out=result[:, features], in_=acc[:])
+                    nc.gpsimd.tensor_tensor(
+                        out=result[:, features], in0=result[:, features], in1=bias, op=ADD
+                    )
+                else:
+                    nc.vector.tensor_tensor(out=result[:, features], in0=acc[:], in1=bias, op=ADD)
+            b, j = divmod(tile_index, LANE_TOKENS)
+            nc.sync.dma_start(out=out_views[w][b, j], in_=result[:])
+
+        grouped_tiles = transpose_half(nc, psum, stage, w_embed_raw, 0, ident, both)
+        quantise_half(nc, grouped_tiles, 0, we_codes, we_scales)
+        grouped_tiles = transpose_half(nc, psum, stage, x_raw, 0, ident, both)
+        quantise_half(nc, grouped_tiles, 0, x_codes, x_scales)
+        transpose_pos(0)
+        embed(0, 0)
+
+        x_tiles = transpose_half(nc, psum, stage, x_raw, HALF, ident, both)
+        we_tiles = transpose_half(nc, psum, stage, w_embed_raw, HALF, ident, both)
+        quantise_half(nc, x_tiles, HALF, x_codes, x_scales)
+        quantise_half(nc, we_tiles, HALF, we_codes, we_scales)
+        later_raws = {}
+        for w in (1, 2):
+            later_raws[w] = raws.tile([P, ROW_TILES * E], BF16, tag="raw", name="later_raw")
+            for half in range(2):
+                load_weight(later_raws[w], w, half)
+        transpose_pos(1)
+        embed(0, 1)
+
+        grouped_tiles = transpose_half(nc, psum, stage, wq_raw, 0, ident, scalar_only)
+        embed(1, 0)
+        quantise_half(nc, grouped_tiles, 0, w_mx[0][0], w_mx[0][1])
+
+        grouped_tiles = transpose_half(nc, psum, stage, wq_raw, HALF, ident, scalar_only)
+        spread_bias(0)
+        quantise_half(nc, grouped_tiles, HALF, w_mx[0][0], w_mx[0][1])
+        embed(1, 1)
+
+        for step in range(HALF):
+            w = 1 + step // 2
+            first_tile = (step % 2) * HALF
+            grouped_tiles = transpose_half(
+                nc, psum, stage, later_raws[w], first_tile, ident, scalar_only
+            )
+            project(0, 2 * step)
+            project(0, 2 * step + 1)
+            quantise_half(nc, grouped_tiles, first_tile, w_mx[w][0], w_mx[w][1])
+            if step % 2 == 1:
+                spread_bias(w)
+        for w in (1, 2):
+            for tile_index in range(ROW_TILES):
+                project(w, tile_index)

@@ -84,6 +84,7 @@ def tile_attention_pa_kernel(
         stage = ctx.enter_context(tc.tile_pool(name="stage", bufs=8))
         outs = ctx.enter_context(tc.tile_pool(name="outs", bufs=6))
         psum = ctx.enter_context(tc.psum_pool(name="psum", bufs=4))
+        ctx.enter_context(tc.manual_schedule())
 
         ident = consts.tile([P, P], F32)
         make_identity(nc, ident[:])

@@ -19,6 +19,7 @@ PASSES = E // K_PASS
 POSITIONS = 512
 TOKENS = 2 * POSITIONS
 ROW_TILES = 8
+PAIRS = ROW_TILES // 2
 HALF = ROW_TILES // 2
 WORDS = E // 2
 BANK = 512
@@ -27,38 +28,34 @@ LANE_TOKENS = 4
 FLOPS = 4 * 2 * TOKENS * E * E
 
 
-def transpose_half(nc, psum, stage, raw, first_tile, ident, copies):
+def transpose_pair(nc, psum, stage, raw, pair, ident):
     raw_words = raw[:].bitcast(F32)
-    banks = {}
-    for pair in range(HALF // 2):
-        for g in range(PASSES):
-            bank = psum.tile([P, 2, 2, P], F32, tag="transposed")
-            for i in range(2):
-                for u in range(2):
-                    first_word = (first_tile + 2 * pair + i) * WORDS + (2 * g + u) * P
-                    nc.tensor.transpose(
-                        bank[:, i, u, :], raw_words[:, first_word : first_word + P], ident[:]
-                    )
-            banks[(pair, g)] = bank
-    grouped_tiles = {}
-    for number, key in enumerate(sorted(banks)):
+    banks = []
+    for g in range(PASSES):
+        bank = psum.tile([P, 2, 2, P], F32, tag="bank")
+        for i in range(2):
+            for u in range(2):
+                first_word = (2 * pair + i) * WORDS + (2 * g + u) * P
+                nc.tensor.transpose(
+                    bank[:, i, u, :], raw_words[:, first_word : first_word + P], ident[:]
+                )
+        banks.append(bank)
+    grouped_tiles = []
+    for bank in banks:
         grouped = stage.tile([P, 2 * P * PACK], BF16, tag="grouped", align_bytes=64)
-        copy = copies[number % len(copies)]
-        copy(
+        nc.scalar.copy(
             out=grouped[:].bitcast(F32).rearrange("p (i r u) -> p i r u", i=2, u=2),
-            in_=banks[key][:].rearrange("p i u r -> p i r u"),
+            in_=bank[:].rearrange("p i u r -> p i r u"),
         )
-        grouped_tiles[key] = grouped
+        grouped_tiles.append(grouped)
     return grouped_tiles
 
 
-def quantise_half(nc, grouped_tiles, first_tile, codes, scales):
-    for pair, g in sorted(grouped_tiles):
-        first = (first_tile + 2 * pair) * P
+def quantise_pair(nc, grouped_tiles, pair, codes, scales):
+    cols = slice(2 * pair * P, 2 * (pair + 1) * P)
+    for g in range(PASSES):
         nc.vector.quantize_mx(
-            out=codes[:, g, first : first + 2 * P].bitcast(FP8X4),
-            scales=scales[:, g, first : first + 2 * P],
-            in_=grouped_tiles[(pair, g)][:],
+            out=codes[:, g, cols].bitcast(FP8X4), scales=scales[:, g, cols], in_=grouped_tiles[g][:]
         )
 
 
@@ -83,7 +80,7 @@ def tile_attention_pa_kernel(
         keep = ctx.enter_context(tc.tile_pool(name="keep", bufs=1))
         stage = ctx.enter_context(tc.tile_pool(name="stage", bufs=8))
         outs = ctx.enter_context(tc.tile_pool(name="outs", bufs=6))
-        psum = ctx.enter_context(tc.psum_pool(name="psum", bufs=4))
+        psum = ctx.enter_context(tc.psum_pool(name="psum", bufs=8))
         ctx.enter_context(tc.manual_schedule())
 
         ident = consts.tile([P, P], F32)
@@ -92,7 +89,7 @@ def tile_attention_pa_kernel(
         nc.vector.memset(ones[:], 1.0)
         bias_rows = consts.tile([P, 3 * E], BF16)
         nc.vector.memset(bias_rows[:], 0.0)
-        b_embed_bf = consts.tile([P, HALF, 2], BF16)
+        b_embed_bf = consts.tile([P, PAIRS, 2], BF16)
         nc.scalar.dma_start(out=b_embed_bf[:], in_=b_embed.rearrange("(a r e) -> r a e", r=P, e=2))
         b_embed_f32 = consts.tile([P, ROW_TILES], F32)
         nc.scalar.activation(
@@ -104,36 +101,36 @@ def tile_attention_pa_kernel(
         wq_raw = raws.tile([P, ROW_TILES * E], BF16, tag="raw")
         pos_raw = consts.tile([P, LANE_TOKENS, E], BF16)
 
-        def load_w_embed(a):
-            nc.sync.dma_start(
-                out=w_embed_raw[:, 2 * a * E : 2 * (a + 1) * E], in_=w_embed_view[:, a, :]
-            )
+        def load_w_embed(pair):
+            cols = slice(2 * pair * E, 2 * (pair + 1) * E)
+            nc.sync.dma_start(out=w_embed_raw[:, cols], in_=w_embed_view[:, pair, :])
 
-        def load_x(b, first_j, count):
-            first = (b * LANE_TOKENS + first_j) * E
+        def load_x(pair):
+            b, half = divmod(pair, 2)
             nc.sync.dma_start(
-                out=x_raw[:, first : first + count * E],
-                in_=x_view[b][:, first_j * E : (first_j + count) * E],
+                out=x_raw[:, 2 * pair * E : 2 * (pair + 1) * E],
+                in_=x_view[b][:, 2 * half * E : 2 * (half + 1) * E],
             )
 
         def load_pos(g_out):
             cols = slice(g_out * K_PASS, (g_out + 1) * K_PASS)
             nc.sync.dma_start(out=pos_raw[:, :, cols], in_=pos_view[:, :, cols])
 
-        def load_weight(raw, w, half):
-            nc.sync.dma_start(
-                out=raw[:, half * HALF * E : (half + 1) * HALF * E].rearrange(
-                    "p (i k) -> p i k", i=HALF
-                ),
-                in_=weight_views[w][:, half * HALF : (half + 1) * HALF, :],
-            )
+        def load_weight(raw, w):
+            for half in range(2):
+                tiles = slice(half * HALF, (half + 1) * HALF)
+                nc.sync.dma_start(
+                    out=raw[:].rearrange("p (i k) -> p i k", i=ROW_TILES)[:, tiles, :],
+                    in_=weight_views[w][:, tiles, :],
+                )
 
         load_w_embed(0)
         load_w_embed(1)
-        load_x(0, 0, 2)
-        load_x(0, 2, 2)
+        load_x(0)
+        load_x(1)
         load_pos(0)
-        load_x(1, 0, LANE_TOKENS)
+        load_x(2)
+        load_x(3)
         load_w_embed(2)
         load_w_embed(3)
         load_pos(1)
@@ -141,27 +138,30 @@ def tile_attention_pa_kernel(
             nc.sync.dma_start(
                 out=bias_rows[0:1, w * E : (w + 1) * E], in_=bias.rearrange("(o f) -> o f", o=1)
             )
-        load_weight(wq_raw, 0, 0)
-        load_weight(wq_raw, 0, 1)
+        load_weight(wq_raw, 0)
 
         def mx_operand(name):
             codes = keep.tile([P, PASSES, E], U32, name=name + "_codes", align_bytes=64)
             scales = keep.tile([P, PASSES, E], U8, name=name + "_scales", align_bytes=64)
             return codes, scales
 
-        x_codes, x_scales = mx_operand("x")
-        we_codes, we_scales = mx_operand("w_embed")
-        xe_codes, xe_scales = mx_operand("xe")
+        x_mx = mx_operand("x")
+        we_mx = mx_operand("w_embed")
+        xe_mx = mx_operand("xe")
         w_mx = [mx_operand(name) for name in ("wq", "wk", "wv")]
 
-        both = (nc.scalar.copy, nc.vector.tensor_copy)
-        scalar_only = (nc.scalar.copy,)
+        def transpose(raw, pairs):
+            return {pair: transpose_pair(nc, psum, stage, raw, pair, ident) for pair in pairs}
+
+        def quantise(grouped, operand):
+            for pair in sorted(grouped):
+                quantise_pair(nc, grouped[pair], pair, operand[0], operand[1])
 
         pos_planes = consts.tile([P, ROW_TILES, POSITIONS], F32)
 
         def transpose_pos(g_out):
             for a in range(2 * g_out, 2 * g_out + 2):
-                bank = psum.tile([P, LANE_TOKENS, P], F32, tag="transposed")
+                bank = psum.tile([P, LANE_TOKENS, P], F32, tag="bank")
                 for j in range(LANE_TOKENS):
                     nc.tensor.transpose(
                         bank[:, j, :], pos_raw[:, j, :].bitcast(F32)[:, a * P : (a + 1) * P], ident[:]
@@ -174,13 +174,22 @@ def tile_attention_pa_kernel(
                 )
                 for e in range(2):
                     plane = 2 * a + e
-                    nc.scalar.activation(
-                        out=pos_planes[:, plane, :],
-                        in_=pairs[:, :, e],
-                        func=IDENTITY,
-                        bias=b_embed_f32[:, plane : plane + 1],
-                        scale=1.0,
-                    )
+                    if a % 2 == 0:
+                        nc.scalar.activation(
+                            out=pos_planes[:, plane, :],
+                            in_=pairs[:, :, e],
+                            func=IDENTITY,
+                            bias=b_embed_f32[:, plane : plane + 1],
+                            scale=1.0,
+                        )
+                    else:
+                        nc.vector.tensor_scalar(
+                            out=pos_planes[:, plane, :],
+                            in0=pairs[:, :, e],
+                            scalar1=b_embed_f32[:, plane : plane + 1],
+                            scalar2=None,
+                            op0=ADD,
+                        )
 
         xe_grouped = keep.tile([P, PASSES, TOKENS * PACK], BF16, align_bytes=64)
 
@@ -188,16 +197,16 @@ def tile_attention_pa_kernel(
             for j in range(LANE_TOKENS):
                 first_token = (LANE_TOKENS * b + j) * P
                 tokens = slice(first_token, first_token + P)
-                acc = psum.tile([P, PACK, P], F32, tag="acc")
+                acc = psum.tile([P, PACK, P], F32, tag="bank")
                 for t in range(PACK):
                     features = slice((PACK * g_out + t) * P, (PACK * g_out + t + 1) * P)
                     for g in range(PASSES):
                         nc.tensor.matmul_mx(
                             out=acc[:, t, :],
-                            lhsT=we_codes[:, g, features].bitcast(FP8X4),
-                            lhsT_scale=we_scales[:, g, features],
-                            rhs=x_codes[:, g, tokens].bitcast(FP8X4),
-                            rhs_scale=x_scales[:, g, tokens],
+                            lhsT=we_mx[0][:, g, features].bitcast(FP8X4),
+                            lhsT_scale=we_mx[1][:, g, features],
+                            rhs=x_mx[0][:, g, tokens].bitcast(FP8X4),
+                            rhs_scale=x_mx[1][:, g, tokens],
                             start=(g == 0),
                             stop=(g == PASSES - 1),
                         )
@@ -213,8 +222,8 @@ def tile_attention_pa_kernel(
                 )
             batch = slice(b * POSITIONS, (b + 1) * POSITIONS)
             nc.vector.quantize_mx(
-                out=xe_codes[:, g_out, batch].bitcast(FP8X4),
-                scales=xe_scales[:, g_out, batch],
+                out=xe_mx[0][:, g_out, batch].bitcast(FP8X4),
+                scales=xe_mx[1][:, g_out, batch],
                 in_=xe_grouped[:, g_out, b * POSITIONS * PACK : (b + 1) * POSITIONS * PACK],
             )
 
@@ -223,7 +232,7 @@ def tile_attention_pa_kernel(
         def spread_bias(w):
             for h in range(E // BANK):
                 cols = slice(w * E + h * BANK, w * E + (h + 1) * BANK)
-                spread = psum.tile([P, BANK], F32, tag="acc")
+                spread = psum.tile([P, BANK], F32, tag="bank")
                 nc.tensor.matmul(
                     spread[:], lhsT=ones[:], rhs=bias_rows[:, cols], start=True, stop=True
                 )
@@ -236,12 +245,12 @@ def tile_attention_pa_kernel(
             for h in range(E // BANK):
                 features = slice(h * BANK, (h + 1) * BANK)
                 bias = bias_all[:, w * E + h * BANK : w * E + (h + 1) * BANK]
-                acc = psum.tile([P, BANK], F32, tag="acc")
+                acc = psum.tile([P, BANK], F32, tag="bank")
                 for g in range(PASSES):
                     nc.tensor.matmul_mx(
                         out=acc[:],
-                        lhsT=xe_codes[:, g, tokens].bitcast(FP8X4),
-                        lhsT_scale=xe_scales[:, g, tokens],
+                        lhsT=xe_mx[0][:, g, tokens].bitcast(FP8X4),
+                        lhsT_scale=xe_mx[1][:, g, tokens],
                         rhs=codes[:, g, features].bitcast(FP8X4),
                         rhs_scale=scales[:, g, features],
                         start=(g == 0),
@@ -258,44 +267,43 @@ def tile_attention_pa_kernel(
             b, j = divmod(tile_index, LANE_TOKENS)
             nc.sync.dma_start(out=out_views[w][b, j], in_=result[:])
 
-        grouped_tiles = transpose_half(nc, psum, stage, w_embed_raw, 0, ident, both)
-        quantise_half(nc, grouped_tiles, 0, we_codes, we_scales)
-        grouped_tiles = transpose_half(nc, psum, stage, x_raw, 0, ident, both)
-        quantise_half(nc, grouped_tiles, 0, x_codes, x_scales)
+        for pair in (0, 1):
+            quantise(transpose(w_embed_raw, [pair]), we_mx)
+        for pair in (0, 1):
+            quantise(transpose(x_raw, [pair]), x_mx)
         transpose_pos(0)
+        x_grouped = transpose(x_raw, [2])
         embed(0, 0)
+        quantise(x_grouped, x_mx)
 
-        x_tiles = transpose_half(nc, psum, stage, x_raw, HALF, ident, both)
-        we_tiles = transpose_half(nc, psum, stage, w_embed_raw, HALF, ident, both)
-        quantise_half(nc, x_tiles, HALF, x_codes, x_scales)
-        quantise_half(nc, we_tiles, HALF, we_codes, we_scales)
+        x_grouped = transpose(x_raw, [3])
+        we_grouped = transpose(w_embed_raw, [2, 3])
+        quantise(x_grouped, x_mx)
+        quantise(we_grouped, we_mx)
         later_raws = {}
         for w in (1, 2):
             later_raws[w] = raws.tile([P, ROW_TILES * E], BF16, tag="raw", name="later_raw")
-            for half in range(2):
-                load_weight(later_raws[w], w, half)
-        transpose_pos(1)
+            load_weight(later_raws[w], w)
         embed(0, 1)
 
-        grouped_tiles = transpose_half(nc, psum, stage, wq_raw, 0, ident, scalar_only)
+        transpose_pos(1)
+        wq_grouped = transpose(wq_raw, [0, 1])
         embed(1, 0)
-        quantise_half(nc, grouped_tiles, 0, w_mx[0][0], w_mx[0][1])
+        quantise(wq_grouped, w_mx[0])
 
-        grouped_tiles = transpose_half(nc, psum, stage, wq_raw, HALF, ident, scalar_only)
+        wq_grouped = transpose(wq_raw, [2, 3])
         spread_bias(0)
-        quantise_half(nc, grouped_tiles, HALF, w_mx[0][0], w_mx[0][1])
+        quantise(wq_grouped, w_mx[0])
         embed(1, 1)
 
-        for step in range(HALF):
+        for step in range(PAIRS):
             w = 1 + step // 2
-            first_tile = (step % 2) * HALF
-            grouped_tiles = transpose_half(
-                nc, psum, stage, later_raws[w], first_tile, ident, scalar_only
-            )
+            half = step % 2
+            w_grouped = transpose(later_raws[w], [2 * half, 2 * half + 1])
             project(0, 2 * step)
             project(0, 2 * step + 1)
-            quantise_half(nc, grouped_tiles, first_tile, w_mx[w][0], w_mx[w][1])
-            if step % 2 == 1:
+            quantise(w_grouped, w_mx[w])
+            if half == 1:
                 spread_bias(w)
         for w in (1, 2):
             for tile_index in range(ROW_TILES):

from contextlib import ExitStack

import concourse.mybir as mybir
from concourse.masks import make_identity

BF16 = mybir.dt.bfloat16
F32 = mybir.dt.float32
U32 = mybir.dt.uint32
U8 = mybir.dt.uint8
FP8X4 = mybir.dt.float8_e4m3fn_x4
ADD = mybir.AluOpType.add
IDENTITY = mybir.ActivationFunctionType.Identity

P = 128
PACK = 4
K_PASS = P * PACK
E = 1024
PASSES = E // K_PASS
POSITIONS = 512
TOKENS = 2 * POSITIONS
ROW_TILES = 8
PAIRS = ROW_TILES // 2
HALF = ROW_TILES // 2
WORDS = E // 2
BANK = 512
LANE_TOKENS = 4

FLOPS = 4 * 2 * TOKENS * E * E


def transpose_pair(nc, psum, stage, raw, pair, ident):
    raw_words = raw[:].bitcast(F32)
    banks = []
    for g in range(PASSES):
        bank = psum.tile([P, 2, 2, P], F32, tag="bank")
        for i in range(2):
            for u in range(2):
                first_word = (2 * pair + i) * WORDS + (2 * g + u) * P
                nc.tensor.transpose(
                    bank[:, i, u, :], raw_words[:, first_word : first_word + P], ident[:]
                )
        banks.append(bank)
    grouped_tiles = []
    for bank in banks:
        grouped = stage.tile([P, 2 * P * PACK], BF16, tag="grouped", align_bytes=64)
        nc.scalar.copy(
            out=grouped[:].bitcast(F32).rearrange("p (i r u) -> p i r u", i=2, u=2),
            in_=bank[:].rearrange("p i u r -> p i r u"),
        )
        grouped_tiles.append(grouped)
    return grouped_tiles


def quantise_pair(nc, grouped_tiles, pair, codes, scales):
    cols = slice(2 * pair * P, 2 * (pair + 1) * P)
    for g in range(PASSES):
        nc.vector.quantize_mx(
            out=codes[:, g, cols].bitcast(FP8X4), scales=scales[:, g, cols], in_=grouped_tiles[g][:]
        )


def tile_attention_pa_kernel(
    tc, x, pos_embed, W_embed, b_embed, Wq, bq, Wk, bk, Wv, bv, out_0, out_1, out_2
):
    nc = tc.nc
    weights = (Wq, Wk, Wv)
    biases = (bq, bk, bv)

    x_view = x.rearrange("b (r j) s d -> b r (j s d)", j=LANE_TOKENS)
    pos_view = pos_embed.rearrange("(r j) e -> r j e", j=LANE_TOKENS)
    out_views = [
        out.rearrange("b (r j) h d -> b j r (h d)", j=LANE_TOKENS) for out in (out_0, out_1, out_2)
    ]
    w_embed_view = W_embed.rearrange("(a r e) k -> r a (e k)", r=P, e=2)
    weight_views = [w.rearrange("(i r) k -> r i k", r=P) for w in weights]

    with ExitStack() as ctx:
        consts = ctx.enter_context(tc.tile_pool(name="consts", bufs=1))
        raws = ctx.enter_context(tc.tile_pool(name="raws", bufs=3))
        keep = ctx.enter_context(tc.tile_pool(name="keep", bufs=1))
        stage = ctx.enter_context(tc.tile_pool(name="stage", bufs=8))
        outs = ctx.enter_context(tc.tile_pool(name="outs", bufs=6))
        psum = ctx.enter_context(tc.psum_pool(name="psum", bufs=8))
        ctx.enter_context(tc.manual_schedule())

        ident = consts.tile([P, P], F32)
        make_identity(nc, ident[:])
        ones = consts.tile([P, P], BF16)
        nc.vector.memset(ones[:], 1.0)
        bias_rows = consts.tile([P, 3 * E], BF16)
        nc.vector.memset(bias_rows[:], 0.0)
        b_embed_bf = consts.tile([P, PAIRS, 2], BF16)
        nc.scalar.dma_start(out=b_embed_bf[:], in_=b_embed.rearrange("(a r e) -> r a e", r=P, e=2))
        b_embed_f32 = consts.tile([P, ROW_TILES], F32)
        nc.scalar.activation(
            out=b_embed_f32[:], in_=b_embed_bf[:].rearrange("p a e -> p (a e)"), func=IDENTITY
        )

        w_embed_raw = raws.tile([P, ROW_TILES * E], BF16, tag="raw")
        x_raw = raws.tile([P, ROW_TILES * E], BF16, tag="raw")
        wq_raw = raws.tile([P, ROW_TILES * E], BF16, tag="raw")
        pos_raw = consts.tile([P, LANE_TOKENS, E], BF16)

        def load_w_embed(pair):
            cols = slice(2 * pair * E, 2 * (pair + 1) * E)
            nc.sync.dma_start(out=w_embed_raw[:, cols], in_=w_embed_view[:, pair, :])

        def load_x(pair):
            b, half = divmod(pair, 2)
            nc.sync.dma_start(
                out=x_raw[:, 2 * pair * E : 2 * (pair + 1) * E],
                in_=x_view[b][:, 2 * half * E : 2 * (half + 1) * E],
            )

        def load_pos(g_out):
            cols = slice(g_out * K_PASS, (g_out + 1) * K_PASS)
            nc.sync.dma_start(out=pos_raw[:, :, cols], in_=pos_view[:, :, cols])

        def load_weight(raw, w):
            for half in range(2):
                tiles = slice(half * HALF, (half + 1) * HALF)
                nc.sync.dma_start(
                    out=raw[:].rearrange("p (i k) -> p i k", i=ROW_TILES)[:, tiles, :],
                    in_=weight_views[w][:, tiles, :],
                )

        load_w_embed(0)
        load_w_embed(1)
        load_x(0)
        load_x(1)
        load_pos(0)
        load_x(2)
        load_x(3)
        load_w_embed(2)
        load_w_embed(3)
        load_pos(1)
        for w, bias in enumerate(biases):
            nc.sync.dma_start(
                out=bias_rows[0:1, w * E : (w + 1) * E], in_=bias.rearrange("(o f) -> o f", o=1)
            )
        load_weight(wq_raw, 0)

        def mx_operand(name):
            codes = keep.tile([P, PASSES, E], U32, name=name + "_codes", align_bytes=64)
            scales = keep.tile([P, PASSES, E], U8, name=name + "_scales", align_bytes=64)
            return codes, scales

        x_mx = mx_operand("x")
        we_mx = mx_operand("w_embed")
        xe_mx = mx_operand("xe")
        w_mx = [mx_operand(name) for name in ("wq", "wk", "wv")]

        def transpose(raw, pairs):
            return {pair: transpose_pair(nc, psum, stage, raw, pair, ident) for pair in pairs}

        def quantise(grouped, operand):
            for pair in sorted(grouped):
                quantise_pair(nc, grouped[pair], pair, operand[0], operand[1])

        pos_planes = consts.tile([P, ROW_TILES, POSITIONS], F32)

        def transpose_pos(g_out):
            for a in range(2 * g_out, 2 * g_out + 2):
                bank = psum.tile([P, LANE_TOKENS, P], F32, tag="bank")
                for j in range(LANE_TOKENS):
                    nc.tensor.transpose(
                        bank[:, j, :], pos_raw[:, j, :].bitcast(F32)[:, a * P : (a + 1) * P], ident[:]
                    )
                pairs = (
                    bank[:]
                    .rearrange("p j r -> p (j r)")
                    .bitcast(BF16)
                    .rearrange("p (c e) -> p c e", e=2)
                )
                for e in range(2):
                    plane = 2 * a + e
                    if a % 2 == 0:
                        nc.scalar.activation(
                            out=pos_planes[:, plane, :],
                            in_=pairs[:, :, e],
                            func=IDENTITY,
                            bias=b_embed_f32[:, plane : plane + 1],
                            scale=1.0,
                        )
                    else:
                        nc.vector.tensor_scalar(
                            out=pos_planes[:, plane, :],
                            in0=pairs[:, :, e],
                            scalar1=b_embed_f32[:, plane : plane + 1],
                            scalar2=None,
                            op0=ADD,
                        )

        xe_grouped = keep.tile([P, PASSES, TOKENS * PACK], BF16, align_bytes=64)

        def embed(g_out, b):
            for j in range(LANE_TOKENS):
                first_token = (LANE_TOKENS * b + j) * P
                tokens = slice(first_token, first_token + P)
                acc = psum.tile([P, PACK, P], F32, tag="bank")
                for t in range(PACK):
                    features = slice((PACK * g_out + t) * P, (PACK * g_out + t + 1) * P)
                    for g in range(PASSES):
                        nc.tensor.matmul_mx(
                            out=acc[:, t, :],
                            lhsT=we_mx[0][:, g, features].bitcast(FP8X4),
                            lhsT_scale=we_mx[1][:, g, features],
                            rhs=x_mx[0][:, g, tokens].bitcast(FP8X4),
                            rhs_scale=x_mx[1][:, g, tokens],
                            start=(g == 0),
                            stop=(g == PASSES - 1),
                        )
                nc.vector.tensor_tensor(
                    out=xe_grouped[
                        :, g_out, first_token * PACK : (first_token + P) * PACK
                    ].rearrange("p (r t) -> p r t", t=PACK),
                    in0=acc[:].rearrange("p t r -> p r t"),
                    in1=pos_planes[
                        :, PACK * g_out : PACK * (g_out + 1), j * P : (j + 1) * P
                    ].rearrange("p t r -> p r t"),
                    op=ADD,
                )
            batch = slice(b * POSITIONS, (b + 1) * POSITIONS)
            nc.vector.quantize_mx(
                out=xe_mx[0][:, g_out, batch].bitcast(FP8X4),
                scales=xe_mx[1][:, g_out, batch],
                in_=xe_grouped[:, g_out, b * POSITIONS * PACK : (b + 1) * POSITIONS * PACK],
            )

        bias_all = consts.tile([P, 3 * E], F32)

        def spread_bias(w):
            for h in range(E // BANK):
                cols = slice(w * E + h * BANK, w * E + (h + 1) * BANK)
                spread = psum.tile([P, BANK], F32, tag="bank")
                nc.tensor.matmul(
                    spread[:], lhsT=ones[:], rhs=bias_rows[:, cols], start=True, stop=True
                )
                nc.scalar.copy(out=bias_all[:, cols], in_=spread[:])

        def project(w, tile_index):
            codes, scales = w_mx[w]
            tokens = slice(tile_index * P, (tile_index + 1) * P)
            result = outs.tile([P, E], F32, tag="result")
            for h in range(E // BANK):
                features = slice(h * BANK, (h + 1) * BANK)
                bias = bias_all[:, w * E + h * BANK : w * E + (h + 1) * BANK]
                acc = psum.tile([P, BANK], F32, tag="bank")
                for g in range(PASSES):
                    nc.tensor.matmul_mx(
                        out=acc[:],
                        lhsT=xe_mx[0][:, g, tokens].bitcast(FP8X4),
                        lhsT_scale=xe_mx[1][:, g, tokens],
                        rhs=codes[:, g, features].bitcast(FP8X4),
                        rhs_scale=scales[:, g, features],
                        start=(g == 0),
                        stop=(g == PASSES - 1),
                    )
                bank_number = (w * ROW_TILES + tile_index) * (E // BANK) + h
                if bank_number % 3 == 0:
                    nc.scalar.copy(out=result[:, features], in_=acc[:])
                    nc.gpsimd.tensor_tensor(
                        out=result[:, features], in0=result[:, features], in1=bias, op=ADD
                    )
                else:
                    nc.vector.tensor_tensor(out=result[:, features], in0=acc[:], in1=bias, op=ADD)
            b, j = divmod(tile_index, LANE_TOKENS)
            nc.sync.dma_start(out=out_views[w][b, j], in_=result[:])

        for pair in (0, 1):
            quantise(transpose(w_embed_raw, [pair]), we_mx)
        for pair in (0, 1):
            quantise(transpose(x_raw, [pair]), x_mx)
        transpose_pos(0)
        x_grouped = transpose(x_raw, [2])
        embed(0, 0)
        quantise(x_grouped, x_mx)

        x_grouped = transpose(x_raw, [3])
        we_grouped = transpose(w_embed_raw, [2, 3])
        quantise(x_grouped, x_mx)
        quantise(we_grouped, we_mx)
        later_raws = {}
        for w in (1, 2):
            later_raws[w] = raws.tile([P, ROW_TILES * E], BF16, tag="raw", name="later_raw")
            load_weight(later_raws[w], w)
        embed(0, 1)

        transpose_pos(1)
        wq_grouped = transpose(wq_raw, [0, 1])
        embed(1, 0)
        quantise(wq_grouped, w_mx[0])

        wq_grouped = transpose(wq_raw, [2, 3])
        spread_bias(0)
        quantise(wq_grouped, w_mx[0])
        embed(1, 1)

        for step in range(PAIRS):
            w = 1 + step // 2
            half = step % 2
            w_grouped = transpose(later_raws[w], [2 * half, 2 * half + 1])
            project(0, 2 * step)
            project(0, 2 * step + 1)
            quantise(w_grouped, w_mx[w])
            if half == 1:
                spread_bias(w)
        for w in (1, 2):
            for tile_index in range(ROW_TILES):
                project(w, tile_index)
